import numpy as np
import ml_dtypes


def mxq(x, axis, fmt="e4m3"):
    dtype, down = {"e4m3": (ml_dtypes.float8_e4m3fn, 7), "e5m2": (ml_dtypes.float8_e5m2, 14)}[fmt]
    v = np.moveaxis(np.asarray(x, np.float32).astype(ml_dtypes.bfloat16).astype(np.float64), axis, -1)
    blocks = v.reshape(v.shape[:-1] + (-1, 32))
    amax = np.abs(blocks).max(-1, keepdims=True)
    byte = np.maximum(np.where(amax > 0, np.frexp(amax)[1] - 1 + 127, 0) - down, 1)
    scale = np.exp2(byte - 127.0)
    codes = (blocks / scale).astype(np.float32).astype(dtype).astype(np.float64)
    return np.moveaxis((codes * scale).reshape(v.shape), -1, axis)


WIDE = False


def mx_kscale(k):
    if not WIDE:
        return np.ones(k)
    levels = np.array([10, -10, 5, -5, 0])
    if k % 512:
        return np.exp2(np.random.permutation(np.resize(levels, k // 32))).repeat(32)
    a = np.empty((k // 512, 16))
    for p in range(k // 512):
        a[p, :8] = np.random.permutation(np.resize(levels, 8))
        for g in range(8):
            far = levels[np.abs(levels - a[p, g]) >= 10]
            a[p, g + 8] = far[np.random.randint(len(far))]
    return np.exp2(a.ravel()).repeat(32)


BF16 = ml_dtypes.bfloat16


def bf(x):
    return np.asarray(x, np.float32).astype(BF16)


def f64(x):
    return np.asarray(x).astype(np.float64)


M, DIN, D = 4096, 128, 512


def setup_inputs():
    s = mx_kscale(D)
    s = s / s.max()
    r = np.random.standard_normal
    return {"S": bf(r((M, D)) * s),
            "X": bf(r((M, DIN))),
            "Uz": bf(r((DIN, D)) * 0.5 / np.sqrt(DIN)),
            "Ug": bf(r((DIN, D)) * 0.5 / np.sqrt(DIN)),
            "Ur": bf(r((DIN, D)) * 0.5 / np.sqrt(DIN)),
            "Uh": bf(r((DIN, D)) * 0.5 / np.sqrt(DIN)),
            "Wz": bf(r((D, D)) * 0.7 / np.sqrt(D) / s[:, None]),
            "Wg": bf(r((D, D)) * 0.7 / np.sqrt(D) / s[:, None]),
            "Wr": bf(r((D, D)) * 0.7 / np.sqrt(D) / s[:, None]),
            "Wh": bf(r((D, D)) * 1.0 / np.sqrt(D) / s[:, None]),
            "bz": bf(r((1, D)) * 0.3),
            "bg": bf(r((1, D)) * 0.3),
            "br": bf(r((1, D)) * 0.3),
            "bh": bf(r((1, D)) * 0.3)}


def reference(S, X, Uz, Ug, Ur, Uh, Wz, Wg, Wr, Wh, bz, bg, br, bh):
    Sf = f64(S)
    Sq = mxq(Sf, 1, "e4m3")
    Z = np.tanh(f64(X) @ f64(Uz) + (Sq @ mxq(f64(Wz), 0, "e4m3")) + f64(bz))
    G = np.tanh(f64(X) @ f64(Ug) + (Sq @ mxq(f64(Wg), 0, "e4m3")) + f64(bg))
    R = np.tanh(f64(X) @ f64(Ur) + (Sq @ mxq(f64(Wr), 0, "e4m3")) + f64(br))
    SR = Sf * R
    H = np.tanh(f64(X) @ f64(Uh) + (mxq(SR, 1, "e4m3") @ mxq(f64(Wh), 0, "e4m3")) + f64(bh))
    return (1.0 - G) * H + Z * Sf

@@ -1,0 +1,332 @@
+from contextlib import ExitStack
+
+import concourse.mybir as mybir
+from concourse.masks import make_identity
+
+F32 = mybir.dt.float32
+BF16 = mybir.dt.bfloat16
+U32 = mybir.dt.uint32
+U8 = mybir.dt.uint8
+FP8X4 = mybir.dt.float8_e4m3fn_x4
+ALU = mybir.AluOpType
+ACT = mybir.ActivationFunctionType
+
+M, DIN, D = 4096, 128, 512
+P = 128
+PACK = 4
+TOKENS = 512
+BLOCKS = 4
+ROUNDS = M // TOKENS
+GATES = ("r", "z", "g", "h")
+
+FLOPS = 2 * M * D * len(GATES) * (D + DIN)
+
+
+def tile_lstmlayer_pa_t_kernel(
+    tc, S, X, Uz, Ug, Ur, Uh, Wz, Wg, Wr, Wh, bz, bg, br, bh, out
+):
+    nc = tc.nc
+    w_dram = {"r": Wr, "z": Wz, "g": Wg, "h": Wh}
+    u_dram = {"r": Ur, "z": Uz, "g": Ug, "h": Uh}
+    b_dram = {"r": br, "z": bz, "g": bg, "h": bh}
+
+    s_rounds = S.rearrange("(s p j) d -> s p j d", p=P, j=BLOCKS)
+    x_rounds = X.rearrange("(s p j) d -> s p j d", p=P, j=BLOCKS)
+    out_rounds = out.rearrange("(s p j) d -> s p j d", p=P, j=BLOCKS)
+
+    with ExitStack() as ctx:
+        ctx.enter_context(tc.manual_schedule())
+        const = ctx.enter_context(tc.tile_pool(name="const", bufs=1))
+        stage = ctx.enter_context(tc.tile_pool(name="stage", bufs=4))
+        loads = ctx.enter_context(tc.tile_pool(name="loads", bufs=3))
+        work = ctx.enter_context(tc.tile_pool(name="work", bufs=2))
+        psum_mx = ctx.enter_context(tc.psum_pool(name="psum_mx", bufs=3))
+        psum_sum = ctx.enter_context(tc.psum_pool(name="psum_sum", bufs=3))
+        psum_t = ctx.enter_context(tc.psum_pool(name="psum_t", bufs=2))
+
+        w_raw = {}
+        u_raw = {}
+        w_codes = {}
+        w_scales = {}
+        u_ready = {}
+        s_nat = {}
+        x_nat = {}
+        s_grouped = {}
+        s_codes = {}
+        s_scales = {}
+        x_t = {}
+        sr_grouped = {}
+        sr_codes = {}
+        sr_scales = {}
+        mx_sb = {}
+        gate_tile = {}
+
+        def load_gate(gate):
+            w_raw[gate] = stage.tile([P, PACK, D], BF16, name="w_raw")
+            nc.sync.dma_start(
+                out=w_raw[gate][:],
+                in_=w_dram[gate].rearrange("(x t) c -> x t c", t=PACK),
+            )
+            u_raw[gate] = const.tile([P, D], BF16, name="u_raw_%s" % gate)
+            nc.sync.dma_start(out=u_raw[gate][:], in_=u_dram[gate])
+
+        def load_round(s):
+            s_nat[s] = loads.tile([P, BLOCKS, D], BF16, name="s_nat")
+            nc.sync.dma_start(out=s_nat[s][:], in_=s_rounds[s])
+            x_nat[s] = loads.tile([P, BLOCKS, DIN], BF16, name="x_nat")
+            nc.sync.dma_start(out=x_nat[s][:], in_=x_rounds[s])
+
+        def prepare_gate(gate):
+            w_grouped = stage.tile([P, D, PACK], BF16, align_bytes=64, bufs=2)
+            if gate == "r":
+                nc.vector.tensor_copy(
+                    out=w_grouped[:].rearrange("x (f c) t -> x f c t", f=PACK),
+                    in_=w_raw[gate][:].rearrange("x t (c f) -> x f c t", f=PACK),
+                )
+                u_ready[gate] = const.tile([P, D], BF16, name="u_sorted")
+                nc.vector.tensor_copy(
+                    out=u_ready[gate][:].rearrange("k (f c) -> k f c", f=PACK),
+                    in_=u_raw[gate][:].rearrange("k (c f) -> k f c", f=PACK),
+                )
+            else:
+                nc.vector.tensor_copy(
+                    out=w_grouped[:], in_=w_raw[gate][:].rearrange("x t c -> x c t")
+                )
+                u_ready[gate] = u_raw[gate]
+            w_codes[gate] = const.tile([P, D], U32, name="w_codes_%s" % gate, align_bytes=64)
+            w_scales[gate] = const.tile([P, D], U8, name="w_scales_%s" % gate, align_bytes=64)
+            nc.vector.quantize_mx(
+                out=w_codes[gate][:].bitcast(FP8X4),
+                scales=w_scales[gate][:],
+                in_=w_grouped[:].rearrange("x c t -> x (c t)"),
+            )
+
+        def bring_in_s(s):
+            s_grouped[s] = work.tile([P, TOKENS, PACK], BF16, name="s_grouped", align_bytes=64)
+            s_words = (
+                s_grouped[s][:]
+                .rearrange("x m t -> x (m t)")
+                .bitcast(F32)
+                .rearrange("x (m u) -> x m u", u=2)
+            )
+            for pair in range(BLOCKS // 2):
+                s_bank = psum_t.tile([P, 2, 2 * P], F32, tag="t")
+                for u in range(2):
+                    for i in range(2):
+                        nc.tensor.transpose(
+                            out=s_bank[:, u, P * i : P * (i + 1)],
+                            in_=s_nat[s][:, 2 * pair + i, :].bitcast(F32)[:, u : 2 * P : 2],
+                            identity=ident_f32[:],
+                        )
+                copy_out(
+                    pair,
+                    s_words[:, 2 * P * pair : 2 * P * (pair + 1), :],
+                    s_bank[:].rearrange("x u m -> x m u"),
+                    None,
+                )
+
+        def bring_in_x(s):
+            x_bank = psum_t.tile([P, TOKENS], BF16, tag="t")
+            for j in range(BLOCKS):
+                nc.tensor.transpose(
+                    out=x_bank[:, P * j : P * (j + 1)], in_=x_nat[s][:, j, :], identity=ident_bf16[:]
+                )
+            x_t[s] = work.tile([P, TOKENS], BF16, name="x_t", bufs=3)
+            copy_out(0, x_t[s][:], x_bank[:], None)
+            s_codes[s] = work.tile([P, TOKENS], U32, name="s_codes", align_bytes=64)
+            s_scales[s] = work.tile([P, TOKENS], U8, name="s_scales", align_bytes=64)
+            nc.vector.quantize_mx(
+                out=s_codes[s][:].bitcast(FP8X4),
+                scales=s_scales[s][:],
+                in_=s_grouped[s][:].rearrange("x m t -> x (m t)"),
+            )
+
+        def copy_out(number, dst, bank, bias):
+            if number % 2 == 0 and bias is None:
+                nc.scalar.copy(out=dst, in_=bank)
+            elif number % 2 == 0:
+                nc.scalar.activation(out=dst, in_=bank, func=ACT.Identity, bias=bias)
+            elif bias is None:
+                nc.vector.tensor_copy(out=dst, in_=bank)
+            else:
+                nc.vector.tensor_scalar_add(out=dst, in0=bank, scalar1=bias)
+
+        def mx_product(gate, s, a):
+            if a == 0:
+                mx_sb[gate, s] = work.tile([P, BLOCKS, TOKENS], F32, name="mx_sb")
+            block = slice(P * a, P * (a + 1))
+            if gate == "h":
+                act_codes, act_scales = sr_codes[s], sr_scales[s]
+            else:
+                act_codes, act_scales = s_codes[s], s_scales[s]
+            mx = psum_mx.tile([P, TOKENS], F32)
+            if gate == "r":
+                nc.tensor.matmul_mx(
+                    out=mx[:],
+                    lhsT=act_codes[:, block].bitcast(FP8X4),
+                    lhsT_scale=act_scales[:, block],
+                    rhs=w_codes[gate][:].bitcast(FP8X4),
+                    rhs_scale=w_scales[gate][:],
+                    start=True,
+                    stop=True,
+                )
+                copy_out(a, mx_sb[gate, s][:, a, :], mx[:], None)
+            else:
+                nc.tensor.matmul_mx(
+                    out=mx[:],
+                    lhsT=w_codes[gate][:, block].bitcast(FP8X4),
+                    lhsT_scale=w_scales[gate][:, block],
+                    rhs=act_codes[:].bitcast(FP8X4),
+                    rhs_scale=act_scales[:],
+                    start=True,
+                    stop=True,
+                )
+                copy_out(a, mx_sb[gate, s][:, a, :], mx[:], bias_col[gate][:, a : a + 1])
+
+        def gate_block(gate, s, b):
+            if b == 0:
+                gate_tile[gate, s] = work.tile(
+                    [P, BLOCKS, TOKENS], F32, name=gate, bufs=3 if gate == "z" else 2
+                )
+            block = slice(P * b, P * (b + 1))
+            total = psum_sum.tile([P, TOKENS], F32)
+            if gate == "r":
+                nc.tensor.matmul(
+                    out=total[:], lhsT=u_ready[gate][:, block], rhs=x_t[s][:], start=True, stop=False
+                )
+            else:
+                nc.tensor.matmul(
+                    out=total[:], lhsT=x_t[s][:, block], rhs=u_ready[gate][:], start=True, stop=False
+                )
+            for a in range(BLOCKS):
+                nc.tensor.matmul(
+                    out=total[:, P * a : P * (a + 1)],
+                    lhsT=mx_sb[gate, s][:, a, block],
+                    rhs=ident_f32[:],
+                    is_transpose=True,
+                    start=False,
+                    stop=(a == BLOCKS - 1),
+                )
+            if gate == "r":
+                nc.scalar.activation(
+                    out=gate_tile[gate, s][:, b, :],
+                    in_=total[:],
+                    func=ACT.Tanh,
+                    bias=bias_col[gate][:, b : b + 1],
+                )
+            else:
+                nc.scalar.activation(out=gate_tile[gate, s][:, b, :], in_=total[:], func=ACT.Tanh)
+
+        def follow_up(gate, s):
+            if gate == "r":
+                sr_grouped[s] = work.tile(
+                    [P, TOKENS, PACK], BF16, name="sr_grouped", align_bytes=64
+                )
+                nc.vector.tensor_tensor(
+                    out=sr_grouped[s][:],
+                    in0=s_grouped[s][:],
+                    in1=gate_tile["r", s][:].rearrange("x t m -> x m t"),
+                    op=ALU.mult,
+                )
+            if gate == "z":
+                nc.vector.tensor_mul(
+                    out=gate_tile["z", s][:], in0=gate_tile["z", s][:], in1=s_nat[s][:]
+                )
+            if gate == "h":
+                nc.vector.scalar_tensor_tensor(
+                    out=gate_tile["g", s][:],
+                    in0=gate_tile["g", s][:],
+                    scalar=1.0,
+                    in1=gate_tile["h", s][:],
+                    op0=ALU.subtract,
+                    op1=ALU.mult,
+                )
+            if gate == "g" and s > 0:
+                finish(s - 1)
+
+        def quantise_sr(s):
+            sr_codes[s] = work.tile([P, TOKENS], U32, name="sr_codes", align_bytes=64)
+            sr_scales[s] = work.tile([P, TOKENS], U8, name="sr_scales", align_bytes=64)
+            nc.vector.quantize_mx(
+                out=sr_codes[s][:].bitcast(FP8X4),
+                scales=sr_scales[s][:],
+                in_=sr_grouped[s][:].rearrange("x m t -> x (m t)"),
+            )
+
+        def finish(s):
+            nc.vector.tensor_sub(
+                out=gate_tile["z", s][:], in0=gate_tile["z", s][:], in1=gate_tile["g", s][:]
+            )
+            nc.sync.dma_start(out=out_rounds[s], in_=gate_tile["z", s][:])
+
+        load_gate("r")
+        load_round(0)
+        bias_rows = const.tile([P, D], BF16)
+        nc.vector.memset(bias_rows[:], 0.0)
+        for index, gate in enumerate(GATES):
+            nc.sync.dma_start(out=bias_rows[index : index + 1, :], in_=b_dram[gate])
+        for gate in ("z", "g", "h"):
+            load_gate(gate)
+        load_round(1)
+
+        ident_f32 = const.tile([P, P], F32)
+        make_identity(nc, ident_f32[:])
+        ident_bf16 = const.tile([P, P], BF16)
+        make_identity(nc, ident_bf16[:])
+
+        prepare_gate("r")
+        bring_in_s(0)
+        bring_in_x(0)
+
+        bias_sorted = const.tile([P, D], BF16)
+        nc.vector.tensor_copy(
+            out=bias_sorted[:].rearrange("k (f c) -> k f c", f=PACK),
+            in_=bias_rows[:].rearrange("k (c f) -> k f c", f=PACK),
+        )
+        bias_col = {}
+        for rows, gates in ((bias_sorted, ("r",)), (bias_rows, ("z", "g", "h"))):
+            bias_bank = psum_t.tile([P, BLOCKS, P], BF16, tag="t")
+            for t in range(BLOCKS):
+                nc.tensor.transpose(
+                    out=bias_bank[:, t, :], in_=rows[:, P * t : P * (t + 1)], identity=ident_bf16[:]
+                )
+            for gate in gates:
+                bias_col[gate] = const.tile([P, BLOCKS], F32, name="bias_col_%s" % gate)
+                nc.vector.tensor_copy(
+                    out=bias_col[gate][:], in_=bias_bank[:, :, GATES.index(gate)]
+                )
+        prepare_gate("z")
+
+        order = [("r", 0)]
+        for s in range(ROUNDS):
+            order.append(("z", s))
+            order.append(("g", s))
+            if s + 1 < ROUNDS:
+                order.append(("r", s + 1))
+            order.append(("h", s))
+
+        for a in range(BLOCKS):
+            mx_product("r", 0, a)
+        for i, (gate, s) in enumerate(order):
+            if gate == "z" and s + 2 < ROUNDS:
+                load_round(s + 2)
+            if i >= 2:
+                follow_up(*order[i - 2])
+            for first in (0, 2):
+                if i + 1 < len(order):
+                    mx_product(*order[i + 1], first)
+                    mx_product(*order[i + 1], first + 1)
+                gate_block(gate, s, first)
+                gate_block(gate, s, first + 1)
+            if i + 3 < len(order) and order[i + 3][0] == "r":
+                bring_in_s(order[i + 3][1])
+            if i + 2 < len(order) and order[i + 2][0] == "r":
+                bring_in_x(order[i + 2][1])
+            if i >= 2 and order[i - 2][0] == "r":
+                quantise_sr(order[i - 2][1])
+            if i < 2:
+                prepare_gate(("g", "h")[i])
+
+        follow_up(*order[len(order) - 2])
+        follow_up(*order[len(order) - 1])
+        finish(ROUNDS - 1)

@@ -40,9 +40,7 @@ def tile_lstmlayer_pa_t_kernel(
         stage = ctx.enter_context(tc.tile_pool(name="stage", bufs=4))
         loads = ctx.enter_context(tc.tile_pool(name="loads", bufs=3))
         work = ctx.enter_context(tc.tile_pool(name="work", bufs=2))
-        psum_mx = ctx.enter_context(tc.psum_pool(name="psum_mx", bufs=3))
-        psum_sum = ctx.enter_context(tc.psum_pool(name="psum_sum", bufs=3))
-        psum_t = ctx.enter_context(tc.psum_pool(name="psum_t", bufs=2))
+        psum = ctx.enter_context(tc.psum_pool(name="psum", bufs=8))
 
         w_raw = {}
         u_raw = {}
@@ -60,6 +58,7 @@ def tile_lstmlayer_pa_t_kernel(
         sr_scales = {}
         mx_sb = {}
         gate_tile = {}
+        sums = {}
 
         def load_gate(gate):
             w_raw[gate] = stage.tile([P, PACK, D], BF16, name="w_raw")
@@ -110,7 +109,7 @@ def tile_lstmlayer_pa_t_kernel(
                 .rearrange("x (m u) -> x m u", u=2)
             )
             for pair in range(BLOCKS // 2):
-                s_bank = psum_t.tile([P, 2, 2 * P], F32, tag="t")
+                s_bank = psum.tile([P, 2, 2 * P], F32, tag="bank")
                 for u in range(2):
                     for i in range(2):
                         nc.tensor.transpose(
@@ -126,7 +125,7 @@ def tile_lstmlayer_pa_t_kernel(
                 )
 
         def bring_in_x(s):
-            x_bank = psum_t.tile([P, TOKENS], BF16, tag="t")
+            x_bank = psum.tile([P, TOKENS], BF16, tag="bank")
             for j in range(BLOCKS):
                 nc.tensor.transpose(
                     out=x_bank[:, P * j : P * (j + 1)], in_=x_nat[s][:, j, :], identity=ident_bf16[:]
@@ -159,7 +158,7 @@ def tile_lstmlayer_pa_t_kernel(
                 act_codes, act_scales = sr_codes[s], sr_scales[s]
             else:
                 act_codes, act_scales = s_codes[s], s_scales[s]
-            mx = psum_mx.tile([P, TOKENS], F32)
+            mx = psum.tile([P, TOKENS], F32, tag="bank")
             if gate == "r":
                 nc.tensor.matmul_mx(
                     out=mx[:],
@@ -183,39 +182,38 @@ def tile_lstmlayer_pa_t_kernel(
                 )
                 copy_out(a, mx_sb[gate, s][:, a, :], mx[:], bias_col[gate][:, a : a + 1])
 
-        def gate_block(gate, s, b):
-            if b == 0:
-                gate_tile[gate, s] = work.tile(
-                    [P, BLOCKS, TOKENS], F32, name=gate, bufs=3 if gate == "z" else 2
-                )
-            block = slice(P * b, P * (b + 1))
-            total = psum_sum.tile([P, TOKENS], F32)
-            if gate == "r":
-                nc.tensor.matmul(
-                    out=total[:], lhsT=u_ready[gate][:, block], rhs=x_t[s][:], start=True, stop=False
-                )
-            else:
-                nc.tensor.matmul(
-                    out=total[:], lhsT=x_t[s][:, block], rhs=u_ready[gate][:], start=True, stop=False
-                )
-            for a in range(BLOCKS):
-                nc.tensor.matmul(
-                    out=total[:, P * a : P * (a + 1)],
-                    lhsT=mx_sb[gate, s][:, a, block],
-                    rhs=ident_f32[:],
-                    is_transpose=True,
-                    start=False,
-                    stop=(a == BLOCKS - 1),
-                )
-            if gate == "r":
-                nc.scalar.activation(
-                    out=gate_tile[gate, s][:, b, :],
-                    in_=total[:],
-                    func=ACT.Tanh,
-                    bias=bias_col[gate][:, b : b + 1],
-                )
-            else:
-                nc.scalar.activation(out=gate_tile[gate, s][:, b, :], in_=total[:], func=ACT.Tanh)
+        def plain_products(gate, s):
+            gate_tile[gate, s] = work.tile(
+                [P, BLOCKS, TOKENS], F32, name=gate, bufs=3 if gate == "z" else 2
+            )
+            for b in range(BLOCKS):
+                block = slice(P * b, P * (b + 1))
+                total = psum.tile([P, TOKENS], F32, tag="bank")
+                sums[b] = total
+                if gate == "r":
+                    lhs_t, rhs = u_ready[gate][:, block], x_t[s][:]
+                else:
+                    lhs_t, rhs = x_t[s][:, block], u_ready[gate][:]
+                nc.tensor.matmul(out=total[:], lhsT=lhs_t, rhs=rhs, start=True, stop=False)
+
+        def finish_gate(gate, s):
+            for b in range(BLOCKS):
+                block = slice(P * b, P * (b + 1))
+                for a in range(BLOCKS):
+                    nc.tensor.matmul(
+                        out=sums[b][:, P * a : P * (a + 1)],
+                        lhsT=mx_sb[gate, s][:, a, block],
+                        rhs=ident_f32[:],
+                        is_transpose=True,
+                        start=False,
+                        stop=(a == BLOCKS - 1),
+                    )
+                out_block = gate_tile[gate, s][:, b, :]
+                if gate == "r":
+                    bias = bias_col[gate][:, b : b + 1]
+                    nc.scalar.activation(out=out_block, in_=sums[b][:], func=ACT.Tanh, bias=bias)
+                else:
+                    nc.scalar.activation(out=out_block, in_=sums[b][:], func=ACT.Tanh)
 
         def follow_up(gate, s):
             if gate == "r":
@@ -285,7 +283,7 @@ def tile_lstmlayer_pa_t_kernel(
         )
         bias_col = {}
         for rows, gates in ((bias_sorted, ("r",)), (bias_rows, ("z", "g", "h"))):
-            bias_bank = psum_t.tile([P, BLOCKS, P], BF16, tag="t")
+            bias_bank = psum.tile([P, BLOCKS, P], BF16, tag="bank")
             for t in range(BLOCKS):
                 nc.tensor.transpose(
                     out=bias_bank[:, t, :], in_=rows[:, P * t : P * (t + 1)], identity=ident_bf16[:]
@@ -312,12 +310,11 @@ def tile_lstmlayer_pa_t_kernel(
                 load_round(s + 2)
             if i >= 2:
                 follow_up(*order[i - 2])
-            for first in (0, 2):
-                if i + 1 < len(order):
-                    mx_product(*order[i + 1], first)
-                    mx_product(*order[i + 1], first + 1)
-                gate_block(gate, s, first)
-                gate_block(gate, s, first + 1)
+            if i + 1 < len(order):
+                for a in range(BLOCKS):
+                    mx_product(*order[i + 1], a)
+            plain_products(gate, s)
+            finish_gate(gate, s)
             if i + 3 < len(order) and order[i + 3][0] == "r":
                 bring_in_s(order[i + 3][1])
             if i + 2 < len(order) and order[i + 2][0] == "r":

@@ -100,29 +100,29 @@ def tile_lstmlayer_pa_t_kernel(
                 in_=w_grouped[:].rearrange("x c t -> x (c t)"),
             )
 
-        def bring_in_s(s):
-            s_grouped[s] = work.tile([P, TOKENS, PACK], BF16, name="s_grouped", align_bytes=64)
+        def bring_in_s(s, pair):
+            if pair == 0:
+                s_grouped[s] = work.tile(
+                    [P, TOKENS, PACK], BF16, name="s_grouped", align_bytes=64
+                )
             s_words = (
                 s_grouped[s][:]
                 .rearrange("x m t -> x (m t)")
                 .bitcast(F32)
                 .rearrange("x (m u) -> x m u", u=2)
             )
-            for pair in range(BLOCKS // 2):
-                s_bank = psum.tile([P, 2, 2 * P], F32, tag="bank")
-                for u in range(2):
-                    for i in range(2):
-                        nc.tensor.transpose(
-                            out=s_bank[:, u, P * i : P * (i + 1)],
-                            in_=s_nat[s][:, 2 * pair + i, :].bitcast(F32)[:, u : 2 * P : 2],
-                            identity=ident_f32[:],
-                        )
-                copy_out(
-                    pair,
-                    s_words[:, 2 * P * pair : 2 * P * (pair + 1), :],
-                    s_bank[:].rearrange("x u m -> x m u"),
-                    None,
-                )
+            s_bank = psum.tile([P, 2, 2 * P], F32, tag="bank")
+            for u in range(2):
+                for i in range(2):
+                    nc.tensor.transpose(
+                        out=s_bank[:, u, P * i : P * (i + 1)],
+                        in_=s_nat[s][:, 2 * pair + i, :].bitcast(F32)[:, u : 2 * P : 2],
+                        identity=ident_f32[:],
+                    )
+            nc.scalar.copy(
+                out=s_words[:, 2 * P * pair : 2 * P * (pair + 1), :],
+                in_=s_bank[:].rearrange("x u m -> x m u"),
+            )
 
         def bring_in_x(s):
             x_bank = psum.tile([P, TOKENS], BF16, tag="bank")
@@ -131,7 +131,7 @@ def tile_lstmlayer_pa_t_kernel(
                     out=x_bank[:, P * j : P * (j + 1)], in_=x_nat[s][:, j, :], identity=ident_bf16[:]
                 )
             x_t[s] = work.tile([P, TOKENS], BF16, name="x_t", bufs=3)
-            copy_out(0, x_t[s][:], x_bank[:], None)
+            nc.scalar.copy(out=x_t[s][:], in_=x_bank[:])
             s_codes[s] = work.tile([P, TOKENS], U32, name="s_codes", align_bytes=64)
             s_scales[s] = work.tile([P, TOKENS], U8, name="s_scales", align_bytes=64)
             nc.vector.quantize_mx(
@@ -196,7 +196,7 @@ def tile_lstmlayer_pa_t_kernel(
                     lhs_t, rhs = x_t[s][:, block], u_ready[gate][:]
                 nc.tensor.matmul(out=total[:], lhsT=lhs_t, rhs=rhs, start=True, stop=False)
 
-        def finish_gate(gate, s):
+        def finish_gate(gate, s, last):
             for b in range(BLOCKS):
                 block = slice(P * b, P * (b + 1))
                 for a in range(BLOCKS):
@@ -214,6 +214,8 @@ def tile_lstmlayer_pa_t_kernel(
                     nc.scalar.activation(out=out_block, in_=sums[b][:], func=ACT.Tanh, bias=bias)
                 else:
                     nc.scalar.activation(out=out_block, in_=sums[b][:], func=ACT.Tanh)
+                if last:
+                    combine(s, b)
 
         def follow_up(gate, s):
             if gate == "r":
@@ -257,6 +259,14 @@ def tile_lstmlayer_pa_t_kernel(
             )
             nc.sync.dma_start(out=out_rounds[s], in_=gate_tile["z", s][:])
 
+        def combine(s, b):
+            z, g, h = gate_tile["z", s][:, b, :], gate_tile["g", s][:, b, :], gate_tile["h", s][:, b, :]
+            nc.vector.scalar_tensor_tensor(
+                out=g, in0=g, scalar=1.0, in1=h, op0=ALU.subtract, op1=ALU.mult
+            )
+            nc.vector.tensor_sub(out=z, in0=z, in1=g)
+            nc.sync.dma_start(out=out_rounds[s][:, b, :], in_=z)
+
         load_gate("r")
         load_round(0)
         bias_rows = const.tile([P, D], BF16)
@@ -273,7 +283,8 @@ def tile_lstmlayer_pa_t_kernel(
         make_identity(nc, ident_bf16[:])
 
         prepare_gate("r")
-        bring_in_s(0)
+        bring_in_s(0, 0)
+        bring_in_s(0, 1)
         bring_in_x(0)
 
         bias_sorted = const.tile([P, D], BF16)
@@ -314,16 +325,19 @@ def tile_lstmlayer_pa_t_kernel(
                 for a in range(BLOCKS):
                     mx_product(*order[i + 1], a)
             plain_products(gate, s)
-            finish_gate(gate, s)
-            if i + 3 < len(order) and order[i + 3][0] == "r":
-                bring_in_s(order[i + 3][1])
-            if i + 2 < len(order) and order[i + 2][0] == "r":
-                bring_in_x(order[i + 2][1])
+            last = i == len(order) - 1
+            if last:
+                follow_up(*order[i - 1])
+            finish_gate(gate, s, last)
+            for s_next in range(1, ROUNDS):
+                first_use = order.index(("r", s_next))
+                if i == max(0, first_use - 4):
+                    bring_in_s(s_next, 0)
+                if i == first_use - 3:
+                    bring_in_s(s_next, 1)
+                if i == first_use - 2:
+                    bring_in_x(s_next)
             if i >= 2 and order[i - 2][0] == "r":
                 quantise_sr(order[i - 2][1])
             if i < 2:
                 prepare_gate(("g", "h")[i])
-
-        follow_up(*order[len(order) - 2])
-        follow_up(*order[len(order) - 1])
-        finish(ROUNDS - 1)

@@ -43,10 +43,10 @@ def tile_lstmlayer_pa_t_kernel(
         psum = ctx.enter_context(tc.psum_pool(name="psum", bufs=8))
 
         w_raw = {}
-        u_raw = {}
+        u_sb = {}
+        w_grouped = {}
         w_codes = {}
         w_scales = {}
-        u_ready = {}
         s_nat = {}
         x_nat = {}
         s_grouped = {}
@@ -60,44 +60,56 @@ def tile_lstmlayer_pa_t_kernel(
         gate_tile = {}
         sums = {}
 
-        def load_gate(gate):
+        def load_w(gate):
             w_raw[gate] = stage.tile([P, PACK, D], BF16, name="w_raw")
             nc.sync.dma_start(
-                out=w_raw[gate][:],
-                in_=w_dram[gate].rearrange("(x t) c -> x t c", t=PACK),
+                out=w_raw[gate][:], in_=w_dram[gate].rearrange("(x t) c -> x t c", t=PACK)
             )
-            u_raw[gate] = const.tile([P, D], BF16, name="u_raw_%s" % gate)
-            nc.sync.dma_start(out=u_raw[gate][:], in_=u_dram[gate])
 
-        def load_round(s):
+        def load_u(gate):
+            u_sb[gate] = const.tile([P, D], BF16, name="u_%s" % gate)
+            nc.sync.dma_start(out=u_sb[gate][:], in_=u_dram[gate])
+
+        def load_s(s, parts):
             s_nat[s] = loads.tile([P, BLOCKS, D], BF16, name="s_nat")
-            nc.sync.dma_start(out=s_nat[s][:], in_=s_rounds[s])
+            for part in range(parts):
+                j = slice(BLOCKS // parts * part, BLOCKS // parts * (part + 1))
+                nc.sync.dma_start(out=s_nat[s][:, j, :], in_=s_rounds[s][:, j, :])
+
+        def load_x(s):
             x_nat[s] = loads.tile([P, BLOCKS, DIN], BF16, name="x_nat")
             nc.sync.dma_start(out=x_nat[s][:], in_=x_rounds[s])
 
-        def prepare_gate(gate):
-            w_grouped = stage.tile([P, D, PACK], BF16, align_bytes=64, bufs=2)
+        def group_gate(gate):
+            w_grouped[gate] = stage.tile([P, D, PACK], BF16, name="w_grouped", align_bytes=64)
             if gate == "r":
                 nc.vector.tensor_copy(
-                    out=w_grouped[:].rearrange("x (f c) t -> x f c t", f=PACK),
+                    out=w_grouped[gate][:].rearrange("x (f c) t -> x f c t", f=PACK),
                     in_=w_raw[gate][:].rearrange("x t (c f) -> x f c t", f=PACK),
                 )
-                u_ready[gate] = const.tile([P, D], BF16, name="u_sorted")
+            elif gate == "z":
                 nc.vector.tensor_copy(
-                    out=u_ready[gate][:].rearrange("k (f c) -> k f c", f=PACK),
-                    in_=u_raw[gate][:].rearrange("k (c f) -> k f c", f=PACK),
+                    out=w_grouped[gate][:], in_=w_raw[gate][:].rearrange("x t c -> x c t")
                 )
             else:
-                nc.vector.tensor_copy(
-                    out=w_grouped[:], in_=w_raw[gate][:].rearrange("x t c -> x c t")
-                )
-                u_ready[gate] = u_raw[gate]
+                for q in range(BLOCKS):
+                    cols = slice(P * q, P * (q + 1))
+                    nc.gpsimd.tensor_scalar(
+                        out=w_grouped[gate][:, cols, :],
+                        in0=w_raw[gate][:, :, cols].rearrange("x t c -> x c t"),
+                        scalar1=1.0,
+                        scalar2=0.0,
+                        op0=ALU.mult,
+                        op1=ALU.add,
+                    )
+
+        def quantise_gate(gate):
             w_codes[gate] = const.tile([P, D], U32, name="w_codes_%s" % gate, align_bytes=64)
             w_scales[gate] = const.tile([P, D], U8, name="w_scales_%s" % gate, align_bytes=64)
             nc.vector.quantize_mx(
                 out=w_codes[gate][:].bitcast(FP8X4),
                 scales=w_scales[gate][:],
-                in_=w_grouped[:].rearrange("x c t -> x (c t)"),
+                in_=w_grouped[gate][:].rearrange("x c t -> x (c t)"),
             )
 
         def bring_in_s(s, pair):
@@ -132,6 +144,8 @@ def tile_lstmlayer_pa_t_kernel(
                 )
             x_t[s] = work.tile([P, TOKENS], BF16, name="x_t", bufs=3)
             nc.scalar.copy(out=x_t[s][:], in_=x_bank[:])
+
+        def quantise_s(s):
             s_codes[s] = work.tile([P, TOKENS], U32, name="s_codes", align_bytes=64)
             s_scales[s] = work.tile([P, TOKENS], U8, name="s_scales", align_bytes=64)
             nc.vector.quantize_mx(
@@ -169,7 +183,7 @@ def tile_lstmlayer_pa_t_kernel(
                     start=True,
                     stop=True,
                 )
-                copy_out(a, mx_sb[gate, s][:, a, :], mx[:], None)
+                copy_out(0 if s == 0 else a, mx_sb[gate, s][:, a, :], mx[:], None)
             else:
                 nc.tensor.matmul_mx(
                     out=mx[:],
@@ -191,9 +205,9 @@ def tile_lstmlayer_pa_t_kernel(
                 total = psum.tile([P, TOKENS], F32, tag="bank")
                 sums[b] = total
                 if gate == "r":
-                    lhs_t, rhs = u_ready[gate][:, block], x_t[s][:]
+                    lhs_t, rhs = u_sb[gate][:, b:D:BLOCKS], x_t[s][:]
                 else:
-                    lhs_t, rhs = x_t[s][:, block], u_ready[gate][:]
+                    lhs_t, rhs = x_t[s][:, block], u_sb[gate][:]
                 nc.tensor.matmul(out=total[:], lhsT=lhs_t, rhs=rhs, start=True, stop=False)
 
         def finish_gate(gate, s, last):
@@ -267,44 +281,57 @@ def tile_lstmlayer_pa_t_kernel(
             nc.vector.tensor_sub(out=z, in0=z, in1=g)
             nc.sync.dma_start(out=out_rounds[s][:, b, :], in_=z)
 
-        load_gate("r")
-        load_round(0)
         bias_rows = const.tile([P, D], BF16)
         nc.vector.memset(bias_rows[:], 0.0)
+        load_w("r")
+        load_s(0, 2)
+        load_w("z")
+        load_x(0)
+        load_u("r")
         for index, gate in enumerate(GATES):
-            nc.sync.dma_start(out=bias_rows[index : index + 1, :], in_=b_dram[gate])
-        for gate in ("z", "g", "h"):
-            load_gate(gate)
-        load_round(1)
+            nc.scalar.dma_start(out=bias_rows[index : index + 1, :], in_=b_dram[gate])
+        load_u("z")
+        load_w("g")
+        load_u("g")
+        load_w("h")
+        load_u("h")
+        load_s(1, 1)
+        load_x(1)
 
         ident_f32 = const.tile([P, P], F32)
         make_identity(nc, ident_f32[:])
         ident_bf16 = const.tile([P, P], BF16)
         make_identity(nc, ident_bf16[:])
 
-        prepare_gate("r")
+        group_gate("r")
+        quantise_gate("r")
         bring_in_s(0, 0)
         bring_in_s(0, 1)
+        quantise_s(0)
+        group_gate("z")
+        quantise_gate("z")
         bring_in_x(0)
+        group_gate("g")
+        group_gate("h")
+        for a in range(BLOCKS):
+            mx_product("r", 0, a)
 
-        bias_sorted = const.tile([P, D], BF16)
-        nc.vector.tensor_copy(
-            out=bias_sorted[:].rearrange("k (f c) -> k f c", f=PACK),
-            in_=bias_rows[:].rearrange("k (c f) -> k f c", f=PACK),
-        )
         bias_col = {}
-        for rows, gates in ((bias_sorted, ("r",)), (bias_rows, ("z", "g", "h"))):
+        for gates in (("z", "g", "h"), ("r",)):
             bias_bank = psum.tile([P, BLOCKS, P], BF16, tag="bank")
             for t in range(BLOCKS):
+                if gates == ("r",):
+                    cols = slice(t, D, BLOCKS)
+                else:
+                    cols = slice(P * t, P * (t + 1))
                 nc.tensor.transpose(
-                    out=bias_bank[:, t, :], in_=rows[:, P * t : P * (t + 1)], identity=ident_bf16[:]
+                    out=bias_bank[:, t, :], in_=bias_rows[:, cols], identity=ident_bf16[:]
                 )
             for gate in gates:
                 bias_col[gate] = const.tile([P, BLOCKS], F32, name="bias_col_%s" % gate)
                 nc.vector.tensor_copy(
                     out=bias_col[gate][:], in_=bias_bank[:, :, GATES.index(gate)]
                 )
-        prepare_gate("z")
 
         order = [("r", 0)]
         for s in range(ROUNDS):
@@ -314,11 +341,10 @@ def tile_lstmlayer_pa_t_kernel(
                 order.append(("r", s + 1))
             order.append(("h", s))
 
-        for a in range(BLOCKS):
-            mx_product("r", 0, a)
         for i, (gate, s) in enumerate(order):
             if gate == "z" and s + 2 < ROUNDS:
-                load_round(s + 2)
+                load_s(s + 2, 1)
+                load_x(s + 2)
             if i >= 2:
                 follow_up(*order[i - 2])
             if i + 1 < len(order):
@@ -337,7 +363,8 @@ def tile_lstmlayer_pa_t_kernel(
                     bring_in_s(s_next, 1)
                 if i == first_use - 2:
                     bring_in_x(s_next)
+                    quantise_s(s_next)
             if i >= 2 and order[i - 2][0] == "r":
                 quantise_sr(order[i - 2][1])
             if i < 2:
-                prepare_gate(("g", "h")[i])
+                quantise_gate(("g", "h")[i])

@@ -88,9 +88,12 @@ def tile_lstmlayer_pa_t_kernel(
                     in_=w_raw[gate][:].rearrange("x t (c f) -> x f c t", f=PACK),
                 )
             elif gate == "z":
-                nc.vector.tensor_copy(
-                    out=w_grouped[gate][:], in_=w_raw[gate][:].rearrange("x t c -> x c t")
-                )
+                for half, copy in enumerate((nc.vector.tensor_copy, nc.scalar.copy)):
+                    cols = slice(D // 2 * half, D // 2 * (half + 1))
+                    copy(
+                        out=w_grouped[gate][:, cols, :],
+                        in_=w_raw[gate][:, :, cols].rearrange("x t c -> x c t"),
+                    )
             else:
                 for q in range(BLOCKS):
                     cols = slice(P * q, P * (q + 1))
@@ -231,32 +234,29 @@ def tile_lstmlayer_pa_t_kernel(
                 if last:
                     combine(s, b)
 
-        def follow_up(gate, s):
-            if gate == "r":
-                sr_grouped[s] = work.tile(
-                    [P, TOKENS, PACK], BF16, name="sr_grouped", align_bytes=64
-                )
-                nc.vector.tensor_tensor(
-                    out=sr_grouped[s][:],
-                    in0=s_grouped[s][:],
-                    in1=gate_tile["r", s][:].rearrange("x t m -> x m t"),
-                    op=ALU.mult,
-                )
-            if gate == "z":
-                nc.vector.tensor_mul(
-                    out=gate_tile["z", s][:], in0=gate_tile["z", s][:], in1=s_nat[s][:]
-                )
-            if gate == "h":
-                nc.vector.scalar_tensor_tensor(
-                    out=gate_tile["g", s][:],
-                    in0=gate_tile["g", s][:],
-                    scalar=1.0,
-                    in1=gate_tile["h", s][:],
-                    op0=ALU.subtract,
-                    op1=ALU.mult,
-                )
-            if gate == "g" and s > 0:
-                finish(s - 1)
+        def s_times_r(s):
+            sr_grouped[s] = work.tile([P, TOKENS, PACK], BF16, name="sr_grouped", align_bytes=64)
+            nc.vector.tensor_tensor(
+                out=sr_grouped[s][:],
+                in0=s_grouped[s][:],
+                in1=gate_tile["r", s][:].rearrange("x t m -> x m t"),
+                op=ALU.mult,
+            )
+
+        def z_times_s(s):
+            nc.vector.tensor_mul(
+                out=gate_tile["z", s][:], in0=gate_tile["z", s][:], in1=s_nat[s][:]
+            )
+
+        def g_times_h(s):
+            nc.vector.scalar_tensor_tensor(
+                out=gate_tile["g", s][:],
+                in0=gate_tile["g", s][:],
+                scalar=1.0,
+                in1=gate_tile["h", s][:],
+                op0=ALU.subtract,
+                op1=ALU.mult,
+            )
 
         def quantise_sr(s):
             sr_codes[s] = work.tile([P, TOKENS], U32, name="sr_codes", align_bytes=64)
@@ -267,10 +267,14 @@ def tile_lstmlayer_pa_t_kernel(
                 in_=sr_grouped[s][:].rearrange("x m t -> x (m t)"),
             )
 
-        def finish(s):
-            nc.vector.tensor_sub(
-                out=gate_tile["z", s][:], in0=gate_tile["z", s][:], in1=gate_tile["g", s][:]
-            )
+        def finish(s, engine):
+            for b in range(BLOCKS):
+                engine.tensor_tensor(
+                    out=gate_tile["z", s][:, b, :],
+                    in0=gate_tile["z", s][:, b, :],
+                    in1=gate_tile["g", s][:, b, :],
+                    op=ALU.subtract,
+                )
             nc.sync.dma_start(out=out_rounds[s], in_=gate_tile["z", s][:])
 
         def combine(s, b):
@@ -285,18 +289,18 @@ def tile_lstmlayer_pa_t_kernel(
         nc.vector.memset(bias_rows[:], 0.0)
         load_w("r")
         load_s(0, 2)
+        for index, gate in enumerate(GATES):
+            nc.sync.dma_start(out=bias_rows[index : index + 1, :], in_=b_dram[gate])
         load_w("z")
         load_x(0)
         load_u("r")
-        for index, gate in enumerate(GATES):
-            nc.scalar.dma_start(out=bias_rows[index : index + 1, :], in_=b_dram[gate])
-        load_u("z")
         load_w("g")
-        load_u("g")
+        load_u("z")
         load_w("h")
-        load_u("h")
+        load_u("g")
         load_s(1, 1)
         load_x(1)
+        load_u("h")
 
         ident_f32 = const.tile([P, P], F32)
         make_identity(nc, ident_f32[:])
@@ -310,11 +314,8 @@ def tile_lstmlayer_pa_t_kernel(
         quantise_s(0)
         group_gate("z")
         quantise_gate("z")
-        bring_in_x(0)
         group_gate("g")
         group_gate("h")
-        for a in range(BLOCKS):
-            mx_product("r", 0, a)
 
         bias_col = {}
         for gates in (("z", "g", "h"), ("r",)):
@@ -333,6 +334,10 @@ def tile_lstmlayer_pa_t_kernel(
                     out=bias_col[gate][:], in_=bias_bank[:, :, GATES.index(gate)]
                 )
 
+        bring_in_x(0)
+        for a in range(BLOCKS):
+            mx_product("r", 0, a)
+
         order = [("r", 0)]
         for s in range(ROUNDS):
             order.append(("z", s))
@@ -342,19 +347,28 @@ def tile_lstmlayer_pa_t_kernel(
             order.append(("h", s))
 
         for i, (gate, s) in enumerate(order):
+            last = i == len(order) - 1
             if gate == "z" and s + 2 < ROUNDS:
                 load_s(s + 2, 1)
                 load_x(s + 2)
-            if i >= 2:
-                follow_up(*order[i - 2])
-            if i + 1 < len(order):
+
+            if i == 2 or (gate == "z" and s > 0):
+                s_times_r(s)
+            elif gate == "g":
+                g_times_h(s - 1)
+                if s < ROUNDS - 1:
+                    finish(s - 1, nc.gpsimd)
+            elif gate == "h":
+                z_times_s(s)
+
+            if not last:
                 for a in range(BLOCKS):
                     mx_product(*order[i + 1], a)
+            if gate == "g" and s == ROUNDS - 1:
+                finish(s - 1, nc.vector)
             plain_products(gate, s)
-            last = i == len(order) - 1
-            if last:
-                follow_up(*order[i - 1])
             finish_gate(gate, s, last)
+
             for s_next in range(1, ROUNDS):
                 first_use = order.index(("r", s_next))
                 if i == max(0, first_use - 4):
@@ -364,7 +378,7 @@ def tile_lstmlayer_pa_t_kernel(
                 if i == first_use - 2:
                     bring_in_x(s_next)
                     quantise_s(s_next)
-            if i >= 2 and order[i - 2][0] == "r":
-                quantise_sr(order[i - 2][1])
+            if i == 2 or (gate == "z" and s > 0):
+                quantise_sr(s)
             if i < 2:
                 quantise_gate(("g", "h")[i])

@@ -237,9 +237,9 @@ def tile_lstmlayer_pa_t_kernel(
         def s_times_r(s):
             sr_grouped[s] = work.tile([P, TOKENS, PACK], BF16, name="sr_grouped", align_bytes=64)
             nc.vector.tensor_tensor(
-                out=sr_grouped[s][:],
-                in0=s_grouped[s][:],
-                in1=gate_tile["r", s][:].rearrange("x t m -> x m t"),
+                out=sr_grouped[s][:].rearrange("x (c i) t -> x c t i", i=4),
+                in0=s_grouped[s][:].rearrange("x (c i) t -> x c t i", i=4),
+                in1=gate_tile["r", s][:].rearrange("x t (c i) -> x c t i", i=4),
                 op=ALU.mult,
             )
 

@@ -197,7 +197,8 @@ def tile_lstmlayer_pa_t_kernel(
                     start=True,
                     stop=True,
                 )
-                copy_out(a, mx_sb[gate, s][:, a, :], mx[:], bias_col[gate][:, a : a + 1])
+                number = 0 if (gate, s) == ("h", ROUNDS - 1) else a
+                copy_out(number, mx_sb[gate, s][:, a, :], mx[:], bias_col[gate][:, a : a + 1])
 
         def plain_products(gate, s):
             gate_tile[gate, s] = work.tile(
@@ -206,33 +207,28 @@ def tile_lstmlayer_pa_t_kernel(
             for b in range(BLOCKS):
                 block = slice(P * b, P * (b + 1))
                 total = psum.tile([P, TOKENS], F32, tag="bank")
-                sums[b] = total
+                sums[gate, b] = total
                 if gate == "r":
                     lhs_t, rhs = u_sb[gate][:, b:D:BLOCKS], x_t[s][:]
                 else:
                     lhs_t, rhs = x_t[s][:, block], u_sb[gate][:]
                 nc.tensor.matmul(out=total[:], lhsT=lhs_t, rhs=rhs, start=True, stop=False)
 
-        def finish_gate(gate, s, last):
-            for b in range(BLOCKS):
-                block = slice(P * b, P * (b + 1))
-                for a in range(BLOCKS):
-                    nc.tensor.matmul(
-                        out=sums[b][:, P * a : P * (a + 1)],
-                        lhsT=mx_sb[gate, s][:, a, block],
-                        rhs=ident_f32[:],
-                        is_transpose=True,
-                        start=False,
-                        stop=(a == BLOCKS - 1),
-                    )
-                out_block = gate_tile[gate, s][:, b, :]
-                if gate == "r":
-                    bias = bias_col[gate][:, b : b + 1]
-                    nc.scalar.activation(out=out_block, in_=sums[b][:], func=ACT.Tanh, bias=bias)
-                else:
-                    nc.scalar.activation(out=out_block, in_=sums[b][:], func=ACT.Tanh)
-                if last:
-                    combine(s, b)
+        def finish_block(gate, s, b):
+            block = slice(P * b, P * (b + 1))
+            for a in range(BLOCKS):
+                nc.tensor.matmul(
+                    out=sums[gate, b][:, P * a : P * (a + 1)],
+                    lhsT=mx_sb[gate, s][:, a, block],
+                    rhs=ident_f32[:],
+                    is_transpose=True,
+                    start=False,
+                    stop=(a == BLOCKS - 1),
+                )
+            bias = bias_col[gate][:, b : b + 1] if gate == "r" else 0.0
+            nc.scalar.activation(
+                out=gate_tile[gate, s][:, b, :], in_=sums[gate, b][:], func=ACT.Tanh, bias=bias
+            )
 
         def s_times_r(s):
             sr_grouped[s] = work.tile([P, TOKENS, PACK], BF16, name="sr_grouped", align_bytes=64)
@@ -277,12 +273,19 @@ def tile_lstmlayer_pa_t_kernel(
                 )
             nc.sync.dma_start(out=out_rounds[s], in_=gate_tile["z", s][:])
 
-        def combine(s, b):
-            z, g, h = gate_tile["z", s][:, b, :], gate_tile["g", s][:, b, :], gate_tile["h", s][:, b, :]
+        def g_times_h_block(s, b):
             nc.vector.scalar_tensor_tensor(
-                out=g, in0=g, scalar=1.0, in1=h, op0=ALU.subtract, op1=ALU.mult
+                out=gate_tile["g", s][:, b, :],
+                in0=gate_tile["g", s][:, b, :],
+                scalar=1.0,
+                in1=gate_tile["h", s][:, b, :],
+                op0=ALU.subtract,
+                op1=ALU.mult,
             )
-            nc.vector.tensor_sub(out=z, in0=z, in1=g)
+
+        def finish_last(s, b):
+            z = gate_tile["z", s][:, b, :]
+            nc.vector.tensor_sub(out=z, in0=z, in1=gate_tile["g", s][:, b, :])
             nc.sync.dma_start(out=out_rounds[s][:, b, :], in_=z)
 
         bias_rows = const.tile([P, D], BF16)
@@ -342,32 +345,55 @@ def tile_lstmlayer_pa_t_kernel(
         for s in range(ROUNDS):
             order.append(("z", s))
             order.append(("g", s))
+            if s == ROUNDS - 2:
+                order.append(("h", s))
             if s + 1 < ROUNDS:
                 order.append(("r", s + 1))
-            order.append(("h", s))
+            if s != ROUNDS - 2:
+                order.append(("h", s))
 
-        for i, (gate, s) in enumerate(order):
-            last = i == len(order) - 1
+        for i, (gate, s) in enumerate(order[:-1]):
+            end = s == ROUNDS - 1
             if gate == "z" and s + 2 < ROUNDS:
                 load_s(s + 2, 1)
                 load_x(s + 2)
 
-            if i == 2 or (gate == "z" and s > 0):
+            if i == 2 or (gate == "z" and 0 < s and not end):
                 s_times_r(s)
-            elif gate == "g":
+            elif gate == "g" and not end:
                 g_times_h(s - 1)
-                if s < ROUNDS - 1:
-                    finish(s - 1, nc.gpsimd)
-            elif gate == "h":
+                finish(s - 1, nc.gpsimd)
+            elif gate == ("g" if end else "h"):
                 z_times_s(s)
 
-            if not last:
-                for a in range(BLOCKS):
-                    mx_product(*order[i + 1], a)
-            if gate == "g" and s == ROUNDS - 1:
+            if gate == "g" and end:
+                plain_products(gate, s)
+            for a in range(BLOCKS):
+                mx_product(*order[i + 1], a)
+
+            if gate == "r" and end:
+                g_times_h(s - 1)
+            elif gate == "z" and end:
+                s_times_r(s)
+                quantise_sr(s)
                 finish(s - 1, nc.vector)
-            plain_products(gate, s)
-            finish_gate(gate, s, last)
+
+            if not (gate == "g" and end):
+                plain_products(gate, s)
+            if gate == "g" and end:
+                for b in (0, 2):
+                    for block in (b, b + 1):
+                        finish_block("g", s, block)
+                    if b == 0:
+                        plain_products("h", s)
+                    for block in (b, b + 1):
+                        finish_block("h", s, block)
+                        g_times_h_block(s, block)
+                    for block in (b, b + 1):
+                        finish_last(s, block)
+            else:
+                for b in range(BLOCKS):
+                    finish_block(gate, s, b)
 
             for s_next in range(1, ROUNDS):
                 first_use = order.index(("r", s_next))
@@ -378,7 +404,7 @@ def tile_lstmlayer_pa_t_kernel(
                 if i == first_use - 2:
                     bring_in_x(s_next)
                     quantise_s(s_next)
-            if i == 2 or (gate == "z" and s > 0):
+            if i == 2 or (gate == "z" and 0 < s and not end):
                 quantise_sr(s)
             if i < 2:
                 quantise_gate(("g", "h")[i])

from contextlib import ExitStack

import concourse.mybir as mybir
from concourse.masks import make_identity

F32 = mybir.dt.float32
BF16 = mybir.dt.bfloat16
U32 = mybir.dt.uint32
U8 = mybir.dt.uint8
FP8X4 = mybir.dt.float8_e4m3fn_x4
ALU = mybir.AluOpType
ACT = mybir.ActivationFunctionType

M, DIN, D = 4096, 128, 512
P = 128
PACK = 4
TOKENS = 512
BLOCKS = 4
ROUNDS = M // TOKENS
GATES = ("r", "z", "g", "h")

FLOPS = 2 * M * D * len(GATES) * (D + DIN)


def tile_lstmlayer_pa_t_kernel(
    tc, S, X, Uz, Ug, Ur, Uh, Wz, Wg, Wr, Wh, bz, bg, br, bh, out
):
    nc = tc.nc
    w_dram = {"r": Wr, "z": Wz, "g": Wg, "h": Wh}
    u_dram = {"r": Ur, "z": Uz, "g": Ug, "h": Uh}
    b_dram = {"r": br, "z": bz, "g": bg, "h": bh}

    s_rounds = S.rearrange("(s p j) d -> s p j d", p=P, j=BLOCKS)
    x_rounds = X.rearrange("(s p j) d -> s p j d", p=P, j=BLOCKS)
    out_rounds = out.rearrange("(s p j) d -> s p j d", p=P, j=BLOCKS)

    with ExitStack() as ctx:
        ctx.enter_context(tc.manual_schedule())
        const = ctx.enter_context(tc.tile_pool(name="const", bufs=1))
        stage = ctx.enter_context(tc.tile_pool(name="stage", bufs=4))
        loads = ctx.enter_context(tc.tile_pool(name="loads", bufs=3))
        work = ctx.enter_context(tc.tile_pool(name="work", bufs=2))
        psum = ctx.enter_context(tc.psum_pool(name="psum", bufs=8))

        w_raw = {}
        u_sb = {}
        w_grouped = {}
        w_codes = {}
        w_scales = {}
        s_nat = {}
        x_nat = {}
        s_grouped = {}
        s_codes = {}
        s_scales = {}
        x_t = {}
        sr_grouped = {}
        sr_codes = {}
        sr_scales = {}
        mx_sb = {}
        gate_tile = {}
        sums = {}

        def load_w(gate):
            w_raw[gate] = stage.tile([P, PACK, D], BF16, name="w_raw")
            nc.sync.dma_start(
                out=w_raw[gate][:], in_=w_dram[gate].rearrange("(x t) c -> x t c", t=PACK)
            )

        def load_u(gate):
            u_sb[gate] = const.tile([P, D], BF16, name="u_%s" % gate)
            nc.sync.dma_start(out=u_sb[gate][:], in_=u_dram[gate])

        def load_s(s, parts):
            s_nat[s] = loads.tile([P, BLOCKS, D], BF16, name="s_nat")
            for part in range(parts):
                j = slice(BLOCKS // parts * part, BLOCKS // parts * (part + 1))
                nc.sync.dma_start(out=s_nat[s][:, j, :], in_=s_rounds[s][:, j, :])

        def load_x(s):
            x_nat[s] = loads.tile([P, BLOCKS, DIN], BF16, name="x_nat")
            nc.sync.dma_start(out=x_nat[s][:], in_=x_rounds[s])

        def group_gate(gate):
            w_grouped[gate] = stage.tile([P, D, PACK], BF16, name="w_grouped", align_bytes=64)
            if gate == "r":
                nc.vector.tensor_copy(
                    out=w_grouped[gate][:].rearrange("x (f c) t -> x f c t", f=PACK),
                    in_=w_raw[gate][:].rearrange("x t (c f) -> x f c t", f=PACK),
                )
            elif gate == "z":
                for half, copy in enumerate((nc.vector.tensor_copy, nc.scalar.copy)):
                    cols = slice(D // 2 * half, D // 2 * (half + 1))
                    copy(
                        out=w_grouped[gate][:, cols, :],
                        in_=w_raw[gate][:, :, cols].rearrange("x t c -> x c t"),
                    )
            else:
                for q in range(BLOCKS):
                    cols = slice(P * q, P * (q + 1))
                    nc.gpsimd.tensor_scalar(
                        out=w_grouped[gate][:, cols, :],
                        in0=w_raw[gate][:, :, cols].rearrange("x t c -> x c t"),
                        scalar1=1.0,
                        scalar2=0.0,
                        op0=ALU.mult,
                        op1=ALU.add,
                    )

        def quantise_gate(gate):
            w_codes[gate] = const.tile([P, D], U32, name="w_codes_%s" % gate, align_bytes=64)
            w_scales[gate] = const.tile([P, D], U8, name="w_scales_%s" % gate, align_bytes=64)
            nc.vector.quantize_mx(
                out=w_codes[gate][:].bitcast(FP8X4),
                scales=w_scales[gate][:],
                in_=w_grouped[gate][:].rearrange("x c t -> x (c t)"),
            )

        def bring_in_s(s, pair):
            if pair == 0:
                s_grouped[s] = work.tile(
                    [P, TOKENS, PACK], BF16, name="s_grouped", align_bytes=64
                )
            s_words = (
                s_grouped[s][:]
                .rearrange("x m t -> x (m t)")
                .bitcast(F32)
                .rearrange("x (m u) -> x m u", u=2)
            )
            s_bank = psum.tile([P, 2, 2 * P], F32, tag="bank")
            for u in range(2):
                for i in range(2):
                    nc.tensor.transpose(
                        out=s_bank[:, u, P * i : P * (i + 1)],
                        in_=s_nat[s][:, 2 * pair + i, :].bitcast(F32)[:, u : 2 * P : 2],
                        identity=ident_f32[:],
                    )
            nc.scalar.copy(
                out=s_words[:, 2 * P * pair : 2 * P * (pair + 1), :],
                in_=s_bank[:].rearrange("x u m -> x m u"),
            )

        def bring_in_x(s):
            x_bank = psum.tile([P, TOKENS], BF16, tag="bank")
            for j in range(BLOCKS):
                nc.tensor.transpose(
                    out=x_bank[:, P * j : P * (j + 1)], in_=x_nat[s][:, j, :], identity=ident_bf16[:]
                )
            x_t[s] = work.tile([P, TOKENS], BF16, name="x_t", bufs=3)
            nc.scalar.copy(out=x_t[s][:], in_=x_bank[:])

        def quantise_s(s):
            s_codes[s] = work.tile([P, TOKENS], U32, name="s_codes", align_bytes=64)
            s_scales[s] = work.tile([P, TOKENS], U8, name="s_scales", align_bytes=64)
            nc.vector.quantize_mx(
                out=s_codes[s][:].bitcast(FP8X4),
                scales=s_scales[s][:],
                in_=s_grouped[s][:].rearrange("x m t -> x (m t)"),
            )

        def copy_out(number, dst, bank, bias):
            if number % 2 == 0 and bias is None:
                nc.scalar.copy(out=dst, in_=bank)
            elif number % 2 == 0:
                nc.scalar.activation(out=dst, in_=bank, func=ACT.Identity, bias=bias)
            elif bias is None:
                nc.vector.tensor_copy(out=dst, in_=bank)
            else:
                nc.vector.tensor_scalar_add(out=dst, in0=bank, scalar1=bias)

        def mx_product(gate, s, a):
            if a == 0:
                mx_sb[gate, s] = work.tile([P, BLOCKS, TOKENS], F32, name="mx_sb")
            block = slice(P * a, P * (a + 1))
            if gate == "h":
                act_codes, act_scales = sr_codes[s], sr_scales[s]
            else:
                act_codes, act_scales = s_codes[s], s_scales[s]
            mx = psum.tile([P, TOKENS], F32, tag="bank")
            if gate == "r":
                nc.tensor.matmul_mx(
                    out=mx[:],
                    lhsT=act_codes[:, block].bitcast(FP8X4),
                    lhsT_scale=act_scales[:, block],
                    rhs=w_codes[gate][:].bitcast(FP8X4),
                    rhs_scale=w_scales[gate][:],
                    start=True,
                    stop=True,
                )
                copy_out(0 if s == 0 else a, mx_sb[gate, s][:, a, :], mx[:], None)
            else:
                nc.tensor.matmul_mx(
                    out=mx[:],
                    lhsT=w_codes[gate][:, block].bitcast(FP8X4),
                    lhsT_scale=w_scales[gate][:, block],
                    rhs=act_codes[:].bitcast(FP8X4),
                    rhs_scale=act_scales[:],
                    start=True,
                    stop=True,
                )
                number = 0 if (gate, s) == ("h", ROUNDS - 1) else a
                copy_out(number, mx_sb[gate, s][:, a, :], mx[:], bias_col[gate][:, a : a + 1])

        def plain_products(gate, s):
            gate_tile[gate, s] = work.tile(
                [P, BLOCKS, TOKENS], F32, name=gate, bufs=3 if gate == "z" else 2
            )
            for b in range(BLOCKS):
                block = slice(P * b, P * (b + 1))
                total = psum.tile([P, TOKENS], F32, tag="bank")
                sums[gate, b] = total
                if gate == "r":
                    lhs_t, rhs = u_sb[gate][:, b:D:BLOCKS], x_t[s][:]
                else:
                    lhs_t, rhs = x_t[s][:, block], u_sb[gate][:]
                nc.tensor.matmul(out=total[:], lhsT=lhs_t, rhs=rhs, start=True, stop=False)

        def finish_block(gate, s, b):
            block = slice(P * b, P * (b + 1))
            for a in range(BLOCKS):
                nc.tensor.matmul(
                    out=sums[gate, b][:, P * a : P * (a + 1)],
                    lhsT=mx_sb[gate, s][:, a, block],
                    rhs=ident_f32[:],
                    is_transpose=True,
                    start=False,
                    stop=(a == BLOCKS - 1),
                )
            bias = bias_col[gate][:, b : b + 1] if gate == "r" else 0.0
            nc.scalar.activation(
                out=gate_tile[gate, s][:, b, :], in_=sums[gate, b][:], func=ACT.Tanh, bias=bias
            )

        def s_times_r(s):
            sr_grouped[s] = work.tile([P, TOKENS, PACK], BF16, name="sr_grouped", align_bytes=64)
            nc.vector.tensor_tensor(
                out=sr_grouped[s][:].rearrange("x (c i) t -> x c t i", i=4),
                in0=s_grouped[s][:].rearrange("x (c i) t -> x c t i", i=4),
                in1=gate_tile["r", s][:].rearrange("x t (c i) -> x c t i", i=4),
                op=ALU.mult,
            )

        def z_times_s(s):
            nc.vector.tensor_mul(
                out=gate_tile["z", s][:], in0=gate_tile["z", s][:], in1=s_nat[s][:]
            )

        def g_times_h(s):
            nc.vector.scalar_tensor_tensor(
                out=gate_tile["g", s][:],
                in0=gate_tile["g", s][:],
                scalar=1.0,
                in1=gate_tile["h", s][:],
                op0=ALU.subtract,
                op1=ALU.mult,
            )

        def quantise_sr(s):
            sr_codes[s] = work.tile([P, TOKENS], U32, name="sr_codes", align_bytes=64)
            sr_scales[s] = work.tile([P, TOKENS], U8, name="sr_scales", align_bytes=64)
            nc.vector.quantize_mx(
                out=sr_codes[s][:].bitcast(FP8X4),
                scales=sr_scales[s][:],
                in_=sr_grouped[s][:].rearrange("x m t -> x (m t)"),
            )

        def finish(s, engine):
            for b in range(BLOCKS):
                engine.tensor_tensor(
                    out=gate_tile["z", s][:, b, :],
                    in0=gate_tile["z", s][:, b, :],
                    in1=gate_tile["g", s][:, b, :],
                    op=ALU.subtract,
                )
            nc.sync.dma_start(out=out_rounds[s], in_=gate_tile["z", s][:])

        def g_times_h_block(s, b):
            nc.vector.scalar_tensor_tensor(
                out=gate_tile["g", s][:, b, :],
                in0=gate_tile["g", s][:, b, :],
                scalar=1.0,
                in1=gate_tile["h", s][:, b, :],
                op0=ALU.subtract,
                op1=ALU.mult,
            )

        def finish_last(s, b):
            z = gate_tile["z", s][:, b, :]
            nc.vector.tensor_sub(out=z, in0=z, in1=gate_tile["g", s][:, b, :])
            nc.sync.dma_start(out=out_rounds[s][:, b, :], in_=z)

        bias_rows = const.tile([P, D], BF16)
        nc.vector.memset(bias_rows[:], 0.0)
        load_w("r")
        load_s(0, 2)
        for index, gate in enumerate(GATES):
            nc.sync.dma_start(out=bias_rows[index : index + 1, :], in_=b_dram[gate])
        load_w("z")
        load_x(0)
        load_u("r")
        load_w("g")
        load_u("z")
        load_w("h")
        load_u("g")
        load_s(1, 1)
        load_x(1)
        load_u("h")

        ident_f32 = const.tile([P, P], F32)
        make_identity(nc, ident_f32[:])
        ident_bf16 = const.tile([P, P], BF16)
        make_identity(nc, ident_bf16[:])

        group_gate("r")
        quantise_gate("r")
        bring_in_s(0, 0)
        bring_in_s(0, 1)
        quantise_s(0)
        group_gate("z")
        quantise_gate("z")
        group_gate("g")
        group_gate("h")

        bias_col = {}
        for gates in (("z", "g", "h"), ("r",)):
            bias_bank = psum.tile([P, BLOCKS, P], BF16, tag="bank")
            for t in range(BLOCKS):
                if gates == ("r",):
                    cols = slice(t, D, BLOCKS)
                else:
                    cols = slice(P * t, P * (t + 1))
                nc.tensor.transpose(
                    out=bias_bank[:, t, :], in_=bias_rows[:, cols], identity=ident_bf16[:]
                )
            for gate in gates:
                bias_col[gate] = const.tile([P, BLOCKS], F32, name="bias_col_%s" % gate)
                nc.vector.tensor_copy(
                    out=bias_col[gate][:], in_=bias_bank[:, :, GATES.index(gate)]
                )

        bring_in_x(0)
        for a in range(BLOCKS):
            mx_product("r", 0, a)

        order = [("r", 0)]
        for s in range(ROUNDS):
            order.append(("z", s))
            order.append(("g", s))
            if s == ROUNDS - 2:
                order.append(("h", s))
            if s + 1 < ROUNDS:
                order.append(("r", s + 1))
            if s != ROUNDS - 2:
                order.append(("h", s))

        for i, (gate, s) in enumerate(order[:-1]):
            end = s == ROUNDS - 1
            if gate == "z" and s + 2 < ROUNDS:
                load_s(s + 2, 1)
                load_x(s + 2)

            if i == 2 or (gate == "z" and 0 < s and not end):
                s_times_r(s)
            elif gate == "g" and not end:
                g_times_h(s - 1)
                finish(s - 1, nc.gpsimd)
            elif gate == ("g" if end else "h"):
                z_times_s(s)

            if gate == "g" and end:
                plain_products(gate, s)
            for a in range(BLOCKS):
                mx_product(*order[i + 1], a)

            if gate == "r" and end:
                g_times_h(s - 1)
            elif gate == "z" and end:
                s_times_r(s)
                quantise_sr(s)
                finish(s - 1, nc.vector)

            if not (gate == "g" and end):
                plain_products(gate, s)
            if gate == "g" and end:
                for b in (0, 2):
                    for block in (b, b + 1):
                        finish_block("g", s, block)
                    if b == 0:
                        plain_products("h", s)
                    for block in (b, b + 1):
                        finish_block("h", s, block)
                        g_times_h_block(s, block)
                    for block in (b, b + 1):
                        finish_last(s, block)
            else:
                for b in range(BLOCKS):
                    finish_block(gate, s, b)

            for s_next in range(1, ROUNDS):
                first_use = order.index(("r", s_next))
                if i == max(0, first_use - 4):
                    bring_in_s(s_next, 0)
                if i == first_use - 3:
                    bring_in_s(s_next, 1)
                if i == first_use - 2:
                    bring_in_x(s_next)
                    quantise_s(s_next)
            if i == 2 or (gate == "z" and 0 < s and not end):
                quantise_sr(s)
            if i < 2:
                quantise_gate(("g", "h")[i])
